import numpy as np
import ml_dtypes


def mxq(x, axis, fmt="e4m3"):
    dtype, down = {"e4m3": (ml_dtypes.float8_e4m3fn, 7), "e5m2": (ml_dtypes.float8_e5m2, 14)}[fmt]
    v = np.moveaxis(np.asarray(x, np.float32).astype(ml_dtypes.bfloat16).astype(np.float64), axis, -1)
    blocks = v.reshape(v.shape[:-1] + (-1, 32))
    amax = np.abs(blocks).max(-1, keepdims=True)
    byte = np.maximum(np.where(amax > 0, np.frexp(amax)[1] - 1 + 127, 0) - down, 1)
    scale = np.exp2(byte - 127.0)
    codes = (blocks / scale).astype(np.float32).astype(dtype).astype(np.float64)
    return np.moveaxis((codes * scale).reshape(v.shape), -1, axis)


WIDE = False


def mx_kscale(k):
    if not WIDE:
        return np.ones(k)
    levels = np.array([30, -30])
    if k % 512:
        return np.exp2(np.random.permutation(np.resize(levels, k // 32))).repeat(32)
    a = np.empty((k // 512, 16))
    for p in range(k // 512):
        a[p, :8] = np.random.permutation(np.resize(levels, 8))
        for g in range(8):
            far = levels[np.abs(levels - a[p, g]) >= 10]
            a[p, g + 8] = far[np.random.randint(len(far))]
    return np.exp2(a.ravel()).repeat(32)


BF16 = ml_dtypes.bfloat16


def bf(x):
    return np.asarray(x, np.float32).astype(BF16)


def f64(x):
    return np.asarray(x).astype(np.float64)


B, S, D, BD, K = 4, 1024, 1024, 512, 128
TS = 3.0


def sigmoid(v):
    return 1.0 / (1.0 + np.exp(-v))


def setup_inputs():
    s = mx_kscale(D)
    return {
        "token_embeddings": bf(np.random.standard_normal((B, S, D)) * TS * s),
        "splat_influences": bf(np.random.uniform(size=(B, S, K))),
        "decoded": bf(np.random.standard_normal((B, K, D)) * 0.35),
        "gate_W": bf(np.random.standard_normal((D, D)) / (TS * np.sqrt(D)) / s[:, None]),
        "gate_b": bf(np.random.standard_normal(D) * 0.5),
    }


def reference(token_embeddings, splat_influences, decoded, gate_W, gate_b):
    flow = f64(splat_influences) @ f64(decoded)
    gate = sigmoid((mxq(f64(token_embeddings), 2, "e5m2") @ mxq(f64(gate_W), 0, "e5m2")) + f64(gate_b))
    return flow * gate

@@ -1,0 +1,284 @@
+from contextlib import ExitStack
+
+import concourse.masks as masks
+import concourse.mybir as mybir
+
+NB, S, D, KS = 4, 1024, 1024, 128
+FLOPS = 2 * NB * S * D * D + 2 * NB * S * KS * D
+
+F32 = mybir.dt.float32
+BF16 = mybir.dt.bfloat16
+U32 = mybir.dt.uint32
+U8 = mybir.dt.uint8
+E5X4 = mybir.dt.float8_e5m2_x4
+ADD = mybir.AluOpType.add
+MULT = mybir.AluOpType.mult
+SIGMOID = mybir.ActivationFunctionType.Sigmoid
+
+P = 128
+NH = 512
+TPB = S // P
+NTILES = NB * TPB
+NPER = NTILES // 2
+PREFETCH = 6
+LEAD = 2
+W_VEC_COLS = 336
+W_LATE = (0, 1)
+OFFLOAD = (2, 3)
+OFF_FROM = 8
+HEAD_TR = (2, 5)
+CP_DELAY = (0, 0)
+QZ_DELAY = 1
+HEAD_H_MAJOR = True
+
+
+def unit_order():
+    units = []
+    first = 0
+    if HEAD_H_MAJOR:
+        for h in range(2):
+            for i in range(4):
+                units.append((i, h))
+        first = 4
+    for i in range(first, NTILES):
+        for h in range(2):
+            units.append((i, h))
+    return units
+
+
+def tile_splatinformationflow_pb_kernel(
+    tc, token_embeddings, splat_influences, decoded, gate_W, gate_b, out
+):
+    nc = tc.nc
+    with ExitStack() as ctx:
+        const = ctx.enter_context(tc.tile_pool(name="const", bufs=1))
+        xin = ctx.enter_context(tc.tile_pool(name="xin", bufs=NPER))
+        batch = ctx.enter_context(tc.tile_pool(name="batch", bufs=NB))
+        wst = ctx.enter_context(tc.tile_pool(name="wst", bufs=4))
+        xq = ctx.enter_context(tc.tile_pool(name="xq", bufs=4))
+        ep = ctx.enter_context(tc.tile_pool(name="ep", bufs=4))
+        psum = ctx.enter_context(tc.psum_pool(name="psum", bufs=3))
+        ctx.enter_context(tc.manual_schedule())
+
+        x_view = [token_embeddings[b].rearrange("(p c) k -> p c k", c=TPB) for b in range(NB)]
+        si_view = [splat_influences[b].rearrange("(p c) s -> p c s", c=TPB) for b in range(NB)]
+        out_view = [out[b].rearrange("(p c) n -> p c n", c=TPB) for b in range(NB)]
+
+        x_t, si_t, dec_t, sit_t, wraw_t = {}, {}, {}, {}, {}
+        xt_t, xg_t, xc_t, xs_t = {}, {}, {}, {}
+        z_t, fl_t, zb_t, o_t = {}, {}, {}, {}
+
+        warm = const.tile([P, 1], F32, name="warm")
+        nc.vector.memset(warm[:], 0.0)
+        nc.scalar.activation(out=warm[:], in_=warm[:], func=SIGMOID)
+        ident_f = const.tile([P, P], F32, name="ident_f")
+        masks.make_identity(nc, ident_f[:])
+        ident_b = const.tile([P, P], BF16, name="ident_b")
+        masks.make_identity(nc, ident_b[:])
+        ones = const.tile([P, P], BF16, name="ones")
+        nc.vector.memset(ones[:], 1.0)
+        brow = const.tile([P, D], BF16, name="brow")
+        nc.vector.memset(brow[:], 0.0)
+        bias_sb = const.tile([P, D], F32, name="bias_sb")
+        wc = const.tile([P, 2, D], U32, name="wc", align_bytes=64)
+        ws = const.tile([P, 2, D], U8, name="ws", align_bytes=64)
+
+        def load_x(j):
+            x = xin.tile([P, 2, D], BF16, name="x", tag="x")
+            b, c = (2 * j) // TPB, (2 * j) % TPB
+            nc.sync.dma_start(out=x[:], in_=x_view[b][:, c : c + 2, :])
+            x_t[j] = x
+
+        def load_w(g, h):
+            wraw = wst.tile([P, 4, NH], BF16, name="wraw", tag="wraw")
+            rows = gate_W[512 * g : 512 * (g + 1), NH * h : NH * (h + 1)]
+            nc.sync.dma_start(out=wraw[:], in_=rows.rearrange("(p j) n -> p j n", j=4))
+            wraw_t[(g, h)] = wraw
+
+        def load_batch(b):
+            si = batch.tile([P, TPB, KS], BF16, name="si", tag="si")
+            nc.sync.dma_start(out=si[:], in_=si_view[b])
+            si_t[b] = si
+            dec = batch.tile([P, D], BF16, name="dec", tag="dec")
+            nc.sync.dma_start(out=dec[:], in_=decoded[b])
+            dec_t[b] = dec
+
+        def prep_w(g, h):
+            wraw = wraw_t[(g, h)]
+            wg = wst.tile([P, NH, 4], BF16, name="wg", tag="wg", bufs=2, align_bytes=64)
+            v = W_VEC_COLS
+            nc.vector.tensor_copy(out=wg[:, :v, :], in_=wraw[:, :, :v].rearrange("p j n -> p n j"))
+            nc.scalar.copy(out=wg[:, v:, :], in_=wraw[:, :, v:].rearrange("p j n -> p n j"))
+            hs = slice(NH * h, NH * (h + 1))
+            nc.vector.quantize_mx(
+                out=wc[:, g, hs].bitcast(E5X4),
+                scales=ws[:, g, hs],
+                in_=wg[:].rearrange("p n j -> p (n j)"),
+            )
+
+        def transpose_x(j):
+            for t in range(2):
+                xt = psum.tile([P, 2, 2, P], F32, name="xt", tag="xt", bufs=2)
+                words = x_t[j][:, t, :].bitcast(F32)
+                for g in range(2):
+                    for u in range(2):
+                        nc.tensor.transpose(
+                            xt[:, g, u, :], words[:, 256 * g + u : 256 * (g + 1) : 2], ident_f[:]
+                        )
+                xt_t[(j, t)] = xt
+
+        def regroup_x(j, t, engine):
+            if t == 0:
+                xg_new = xq.tile([P, 2, D], BF16, name="xg", tag="xg", align_bytes=64)
+                xg_t[j] = xg_new
+            dst = xg_t[j][:, t, :].bitcast(F32).rearrange("p (g r u) -> p g r u", g=2, u=2)
+            src = xt_t[(j, t)][:].rearrange("p g u r -> p g r u")
+            if engine == "v":
+                nc.vector.tensor_copy(out=dst, in_=src)
+            else:
+                nc.scalar.copy(out=dst, in_=src)
+
+        def quantize_x(j):
+            xc = xq.tile([P, 4 * P], U32, name="xc", tag="xc", align_bytes=64)
+            xs = xq.tile([P, 4 * P], U8, name="xs", tag="xs", align_bytes=64)
+            nc.vector.quantize_mx(
+                out=xc[:].bitcast(E5X4), scales=xs[:], in_=xg_t[j][:].rearrange("p t c -> p (t c)")
+            )
+            xc_t[j] = xc
+            xs_t[j] = xs
+
+        def transpose_si(b):
+            sp = psum.tile([P, TPB, P], BF16, name="sp", tag="fl")
+            for c in range(TPB):
+                nc.tensor.transpose(sp[:, c, :], si_t[b][:, c, :], ident_b[:])
+            sit = batch.tile([P, TPB, P], BF16, name="sit", tag="sit")
+            nc.scalar.copy(out=sit[:], in_=sp[:])
+            sit_t[b] = sit
+
+        def spread_bias():
+            for h in range(2):
+                hs = slice(NH * h, NH * (h + 1))
+                bp = psum.tile([P, NH], F32, name="bp", tag="z")
+                nc.tensor.matmul(out=bp[:], lhsT=ones[:], rhs=brow[:, hs], start=True, stop=True)
+                nc.scalar.copy(out=bias_sb[:, hs], in_=bp[:])
+
+        def gate_matmul(u):
+            i, h = u
+            j, t = i // 2, i % 2
+            hs = slice(NH * h, NH * (h + 1))
+            z = psum.tile([P, NH], F32, name="z", tag="z")
+            for g in range(2):
+                cols = slice((2 * t + g) * P, (2 * t + g + 1) * P)
+                nc.tensor.matmul_mx(
+                    out=z[:],
+                    lhsT=xc_t[j][:, cols].bitcast(E5X4),
+                    lhsT_scale=xs_t[j][:, cols],
+                    rhs=wc[:, g, hs].bitcast(E5X4),
+                    rhs_scale=ws[:, g, hs],
+                    start=(g == 0),
+                    stop=(g == 1),
+                )
+            z_t[u] = z
+
+        def flow_matmul(u):
+            i, h = u
+            b, c = i // TPB, i % TPB
+            fl = psum.tile([P, NH], F32, name="fl", tag="fl")
+            nc.tensor.matmul(
+                out=fl[:], lhsT=sit_t[b][:, c, :], rhs=dec_t[b][:, NH * h : NH * (h + 1)], start=True, stop=True
+            )
+            fl_t[u] = fl
+
+        def add_bias(u):
+            h = u[1]
+            zb = ep.tile([P, NH], F32, name="zb", tag="zb")
+            nc.vector.tensor_tensor(out=zb[:], in0=z_t[u][:], in1=bias_sb[:, NH * h : NH * (h + 1)], op=ADD)
+            zb_t[u] = zb
+
+        def sigmoid(u):
+            nc.scalar.activation(out=zb_t[u][:], in_=zb_t[u][:], func=SIGMOID)
+
+        def product(u, n):
+            i, h = u
+            if i not in o_t:
+                o_new = ep.tile([P, D], F32, name="o", tag="o", bufs=8)
+                o_t[i] = o_new
+            dst = o_t[i][:, NH * h : NH * (h + 1)]
+            if n % 4 in OFFLOAD and n >= OFF_FROM:
+                fs = ep.tile([P, NH], F32, name="fs", tag="fs", bufs=2)
+                nc.scalar.copy(out=fs[:], in_=fl_t[u][:])
+                nc.gpsimd.tensor_tensor(out=dst, in0=zb_t[u][:], in1=fs[:], op=MULT)
+            else:
+                nc.vector.tensor_tensor(out=dst, in0=fl_t[u][:], in1=zb_t[u][:], op=MULT)
+
+        def store(i):
+            b, c = i // TPB, i % TPB
+            nc.sync.dma_start(out=out_view[b][:, c, :], in_=o_t[i][:])
+
+        load_x(0)
+        load_w(0, 0)
+        load_w(1, 0)
+        load_x(1)
+        nc.sync.dma_start(out=brow[0:1, :], in_=gate_b.rearrange("(o n) -> o n", o=1))
+        load_batch(0)
+        load_w(0, 1)
+        load_w(1, 1)
+        for j in range(2, PREFETCH):
+            load_x(j)
+
+        transpose_x(0)
+        regroup_x(0, 0, "v")
+        regroup_x(0, 1, "s")
+        prep_w(0, 0)
+        quantize_x(0)
+        prep_w(1, 0)
+        transpose_x(1)
+        regroup_x(1, 0, "s")
+        regroup_x(1, 1, "s")
+        spread_bias()
+        quantize_x(1)
+
+        units = unit_order()
+        tr_at = {}
+        for j in range(2, NPER):
+            tr_at[HEAD_TR[j - 2] if j - 2 < len(HEAD_TR) else 4 * (j - LEAD)] = j
+        late = {W_LATE[0]: (0, 1), W_LATE[1]: (1, 1)}
+        done_halves = {}
+        for n in range(len(units) + 1):
+            u = units[n] if n < len(units) else None
+            up = units[n - 1] if n >= 1 else None
+            if n % 4 == 0:
+                j = n // 4
+                if j + PREFETCH < NPER:
+                    load_x(j + PREFETCH)
+                if j % 4 == 0 and j // 4 + 1 < NB:
+                    load_batch(j // 4 + 1)
+            if n in tr_at:
+                transpose_x(tr_at[n])
+                if tr_at[n] % 4 == 0:
+                    transpose_si(tr_at[n] // 4)
+            if u is not None:
+                gate_matmul(u)
+                if n == 0:
+                    transpose_si(0)
+            if up is not None:
+                flow_matmul(up)
+            if u is not None:
+                add_bias(u)
+            if up is not None:
+                product(up, n)
+            if u is not None:
+                sigmoid(u)
+            if n - CP_DELAY[0] in tr_at:
+                regroup_x(tr_at[n - CP_DELAY[0]], 0, "s")
+            if n - CP_DELAY[1] in tr_at:
+                regroup_x(tr_at[n - CP_DELAY[1]], 1, "s")
+            if up is not None:
+                i = up[0]
+                done_halves[i] = done_halves.get(i, 0) + 1
+                if done_halves[i] == 2:
+                    store(i)
+            if n - QZ_DELAY in tr_at:
+                quantize_x(tr_at[n - QZ_DELAY])
+            if n in late:
+                prep_w(late[n][0], late[n][1])

@@ -23,24 +23,48 @@ NPER = NTILES // 2
 PREFETCH = 6
 LEAD = 2
 W_VEC_COLS = 336
-W_LATE = (0, 1)
-OFFLOAD = (2, 3)
-OFF_FROM = 8
-HEAD_TR = (2, 5)
+W_LATE = (4, 6)
+OFF_MOD = 8
+OFFLOAD = (1, 4, 6)
+OFF_HEAD = (1, 4, 6)
+OFF_TAIL = (0, 2, 4, 6)
+TAIL_FROM = 52
+HEAD_TR = (1, 3)
+SIT0_AT = 0
 CP_DELAY = (0, 0)
-QZ_DELAY = 1
-HEAD_H_MAJOR = True
+QZ_DELAY = 3
+LAG_F = 2
+LAG_P = 2
+ZB_BUFS = 6
+FS_BUFS = 2
+HM = 8
+OFF_LAST = 2
+O_BUFS = 10
+QZ_HEAD = 1
+XQ_BUFS = 6
+Z_BUFS = 3
+FL_BUFS = 3
+XT_BUFS = 2
+TR_PAIR = False
+CP_EARLY = True
+W_GP = True
+TR_SHIFT = 0
+
+
+def offloaded(m):
+    if m < 16:
+        return m % 8 in OFF_HEAD
+    if m < TAIL_FROM:
+        return m % 8 in OFFLOAD
+    return m % 8 in OFF_TAIL and m < 2 * NTILES - OFF_LAST
 
 
 def unit_order():
     units = []
-    first = 0
-    if HEAD_H_MAJOR:
-        for h in range(2):
-            for i in range(4):
-                units.append((i, h))
-        first = 4
-    for i in range(first, NTILES):
+    for h in range(2):
+        for i in range(HM):
+            units.append((i, h))
+    for i in range(HM, NTILES):
         for h in range(2):
             units.append((i, h))
     return units
@@ -55,9 +79,9 @@ def tile_splatinformationflow_pb_kernel(
         xin = ctx.enter_context(tc.tile_pool(name="xin", bufs=NPER))
         batch = ctx.enter_context(tc.tile_pool(name="batch", bufs=NB))
         wst = ctx.enter_context(tc.tile_pool(name="wst", bufs=4))
-        xq = ctx.enter_context(tc.tile_pool(name="xq", bufs=4))
+        xq = ctx.enter_context(tc.tile_pool(name="xq", bufs=XQ_BUFS))
         ep = ctx.enter_context(tc.tile_pool(name="ep", bufs=4))
-        psum = ctx.enter_context(tc.psum_pool(name="psum", bufs=3))
+        psum = ctx.enter_context(tc.psum_pool(name="psum", bufs=Z_BUFS))
         ctx.enter_context(tc.manual_schedule())
 
         x_view = [token_embeddings[b].rearrange("(p c) k -> p c k", c=TPB) for b in range(NB)]
@@ -67,6 +91,7 @@ def tile_splatinformationflow_pb_kernel(
         x_t, si_t, dec_t, sit_t, wraw_t = {}, {}, {}, {}, {}
         xt_t, xg_t, xc_t, xs_t = {}, {}, {}, {}
         z_t, fl_t, zb_t, o_t = {}, {}, {}, {}
+        wg_t = {}
 
         warm = const.tile([P, 1], F32, name="warm")
         nc.vector.memset(warm[:], 0.0)
@@ -103,22 +128,32 @@ def tile_splatinformationflow_pb_kernel(
             nc.sync.dma_start(out=dec[:], in_=decoded[b])
             dec_t[b] = dec
 
-        def prep_w(g, h):
+        def interleave_w(g, h):
             wraw = wraw_t[(g, h)]
             wg = wst.tile([P, NH, 4], BF16, name="wg", tag="wg", bufs=2, align_bytes=64)
             v = W_VEC_COLS
             nc.vector.tensor_copy(out=wg[:, :v, :], in_=wraw[:, :, :v].rearrange("p j n -> p n j"))
             nc.scalar.copy(out=wg[:, v:, :], in_=wraw[:, :, v:].rearrange("p j n -> p n j"))
+            wg_t[(g, h)] = wg
+
+        def interleave_w_gpsimd(g, h):
+            wg = wst.tile([P, NH, 4], BF16, name="wg", tag="wg", bufs=2, align_bytes=64)
+            nc.gpsimd.tensor_scalar(
+                out=wg[:], in0=wraw_t[(g, h)][:].rearrange("p j n -> p n j"), scalar1=1.0, scalar2=0.0, op0=MULT, op1=ADD
+            )
+            wg_t[(g, h)] = wg
+
+        def quantize_w(g, h):
             hs = slice(NH * h, NH * (h + 1))
             nc.vector.quantize_mx(
                 out=wc[:, g, hs].bitcast(E5X4),
                 scales=ws[:, g, hs],
-                in_=wg[:].rearrange("p n j -> p (n j)"),
+                in_=wg_t[(g, h)][:].rearrange("p n j -> p (n j)"),
             )
 
         def transpose_x(j):
             for t in range(2):
-                xt = psum.tile([P, 2, 2, P], F32, name="xt", tag="xt", bufs=2)
+                xt = psum.tile([P, 2, 2, P], F32, name="xt", tag="xt", bufs=XT_BUFS)
                 words = x_t[j][:, t, :].bitcast(F32)
                 for g in range(2):
                     for u in range(2):
@@ -129,7 +164,7 @@ def tile_splatinformationflow_pb_kernel(
 
         def regroup_x(j, t, engine):
             if t == 0:
-                xg_new = xq.tile([P, 2, D], BF16, name="xg", tag="xg", align_bytes=64)
+                xg_new = xq.tile([P, 2, D], BF16, name="xg", tag="xg", bufs=3, align_bytes=64)
                 xg_t[j] = xg_new
             dst = xg_t[j][:, t, :].bitcast(F32).rearrange("p (g r u) -> p g r u", g=2, u=2)
             src = xt_t[(j, t)][:].rearrange("p g u r -> p g r u")
@@ -148,7 +183,7 @@ def tile_splatinformationflow_pb_kernel(
             xs_t[j] = xs
 
         def transpose_si(b):
-            sp = psum.tile([P, TPB, P], BF16, name="sp", tag="fl")
+            sp = psum.tile([P, TPB, P], BF16, name="sp", tag="fl", bufs=FL_BUFS)
             for c in range(TPB):
                 nc.tensor.transpose(sp[:, c, :], si_t[b][:, c, :], ident_b[:])
             sit = batch.tile([P, TPB, P], BF16, name="sit", tag="sit")
@@ -183,7 +218,7 @@ def tile_splatinformationflow_pb_kernel(
         def flow_matmul(u):
             i, h = u
             b, c = i // TPB, i % TPB
-            fl = psum.tile([P, NH], F32, name="fl", tag="fl")
+            fl = psum.tile([P, NH], F32, name="fl", tag="fl", bufs=FL_BUFS)
             nc.tensor.matmul(
                 out=fl[:], lhsT=sit_t[b][:, c, :], rhs=dec_t[b][:, NH * h : NH * (h + 1)], start=True, stop=True
             )
@@ -191,7 +226,7 @@ def tile_splatinformationflow_pb_kernel(
 
         def add_bias(u):
             h = u[1]
-            zb = ep.tile([P, NH], F32, name="zb", tag="zb")
+            zb = ep.tile([P, NH], F32, name="zb", tag="zb", bufs=ZB_BUFS)
             nc.vector.tensor_tensor(out=zb[:], in0=z_t[u][:], in1=bias_sb[:, NH * h : NH * (h + 1)], op=ADD)
             zb_t[u] = zb
 
@@ -201,11 +236,11 @@ def tile_splatinformationflow_pb_kernel(
         def product(u, n):
             i, h = u
             if i not in o_t:
-                o_new = ep.tile([P, D], F32, name="o", tag="o", bufs=8)
+                o_new = ep.tile([P, D], F32, name="o", tag="o", bufs=O_BUFS)
                 o_t[i] = o_new
             dst = o_t[i][:, NH * h : NH * (h + 1)]
-            if n % 4 in OFFLOAD and n >= OFF_FROM:
-                fs = ep.tile([P, NH], F32, name="fs", tag="fs", bufs=2)
+            if offloaded(n - LAG_P):
+                fs = ep.tile([P, NH], F32, name="fs", tag="fs", bufs=FS_BUFS)
                 nc.scalar.copy(out=fs[:], in_=fl_t[u][:])
                 nc.gpsimd.tensor_tensor(out=dst, in0=zb_t[u][:], in1=fs[:], op=MULT)
             else:
@@ -221,64 +256,90 @@ def tile_splatinformationflow_pb_kernel(
         load_x(1)
         nc.sync.dma_start(out=brow[0:1, :], in_=gate_b.rearrange("(o n) -> o n", o=1))
         load_batch(0)
+        load_x(2)
+        load_x(3)
         load_w(0, 1)
         load_w(1, 1)
-        for j in range(2, PREFETCH):
+        for j in range(4, PREFETCH):
             load_x(j)
+        load_batch(1)
 
         transpose_x(0)
         regroup_x(0, 0, "v")
         regroup_x(0, 1, "s")
-        prep_w(0, 0)
+        interleave_w(0, 0)
+        interleave_w(1, 0)
+        quantize_w(0, 0)
         quantize_x(0)
-        prep_w(1, 0)
+        quantize_w(1, 0)
         transpose_x(1)
         regroup_x(1, 0, "s")
         regroup_x(1, 1, "s")
         spread_bias()
         quantize_x(1)
 
+        if W_GP:
+            interleave_w_gpsimd(0, 1)
+            interleave_w_gpsimd(1, 1)
+
         units = unit_order()
         tr_at = {}
         for j in range(2, NPER):
-            tr_at[HEAD_TR[j - 2] if j - 2 < len(HEAD_TR) else 4 * (j - LEAD)] = j
+            if j - 2 < len(HEAD_TR):
+                tr_at[HEAD_TR[j - 2]] = [j]
+            elif TR_PAIR:
+                tr_at.setdefault(8 * ((j - LEAD) // 2) - TR_SHIFT, []).append(j)
+            else:
+                tr_at[4 * (j - LEAD)] = [j]
         late = {W_LATE[0]: (0, 1), W_LATE[1]: (1, 1)}
         done_halves = {}
-        for n in range(len(units) + 1):
+        for n in range(len(units) + LAG_P):
             u = units[n] if n < len(units) else None
-            up = units[n - 1] if n >= 1 else None
+            uf = units[n - LAG_F] if 0 <= n - LAG_F < len(units) else None
+            up = units[n - LAG_P] if n >= LAG_P else None
             if n % 4 == 0:
                 j = n // 4
                 if j + PREFETCH < NPER:
                     load_x(j + PREFETCH)
-                if j % 4 == 0 and j // 4 + 1 < NB:
-                    load_batch(j // 4 + 1)
-            if n in tr_at:
-                transpose_x(tr_at[n])
-                if tr_at[n] % 4 == 0:
-                    transpose_si(tr_at[n] // 4)
+                if j % 4 == 0 and j // 4 + 2 < NB:
+                    load_batch(j // 4 + 2)
+            for j in tr_at.get(n, []):
+                transpose_x(j)
+                if j % 4 == 0:
+                    transpose_si(j // 4)
+                if CP_EARLY:
+                    regroup_x(j, 0, "s")
+                    regroup_x(j, 1, "s")
             if u is not None:
                 gate_matmul(u)
-                if n == 0:
+                if n == SIT0_AT:
                     transpose_si(0)
-            if up is not None:
-                flow_matmul(up)
+            if uf is not None:
+                flow_matmul(uf)
             if u is not None:
                 add_bias(u)
             if up is not None:
                 product(up, n)
             if u is not None:
                 sigmoid(u)
-            if n - CP_DELAY[0] in tr_at:
-                regroup_x(tr_at[n - CP_DELAY[0]], 0, "s")
-            if n - CP_DELAY[1] in tr_at:
-                regroup_x(tr_at[n - CP_DELAY[1]], 1, "s")
+            for j in tr_at.get(n - CP_DELAY[0], [])[: (0 if CP_EARLY else 1)]:
+                regroup_x(j, 0, "s")
+                regroup_x(j, 1, "s")
+            for j in tr_at.get(n - CP_DELAY[1], [])[1:]:
+                regroup_x(j, 0, "s")
+                regroup_x(j, 1, "s")
             if up is not None:
                 i = up[0]
                 done_halves[i] = done_halves.get(i, 0) + 1
                 if done_halves[i] == 2:
                     store(i)
-            if n - QZ_DELAY in tr_at:
-                quantize_x(tr_at[n - QZ_DELAY])
+            for j in tr_at.get(n - QZ_HEAD, []):
+                if j < 4:
+                    quantize_x(j)
+            for j in tr_at.get(n - QZ_DELAY, [])[:1]:
+                if j >= 4:
+                    quantize_x(j)
+            for j in tr_at.get(n - QZ_DELAY - 2, [])[1:]:
+                quantize_x(j)
             if n in late:
-                prep_w(late[n][0], late[n][1])
+                quantize_w(late[n][0], late[n][1])

@@ -31,6 +31,14 @@ OFF_TAIL = (0, 2, 4, 6)
 TAIL_FROM = 52
 HEAD_TR = (1, 3)
 SIT0_AT = 0
+WL_BEFORE = 4
+DEINT = ()
+XD_BUFS = 4
+DE_FROM = 4
+DE_LEAD = 4
+GP_SPLIT = 4
+WG_SPLIT = 8
+QZ_MID = False
 CP_DELAY = (0, 0)
 QZ_DELAY = 3
 LAG_F = 2
@@ -92,6 +100,7 @@ def tile_splatinformationflow_pb_kernel(
         xt_t, xg_t, xc_t, xs_t = {}, {}, {}, {}
         z_t, fl_t, zb_t, o_t = {}, {}, {}, {}
         wg_t = {}
+        xd_t = {}
 
         warm = const.tile([P, 1], F32, name="warm")
         nc.vector.memset(warm[:], 0.0)
@@ -138,9 +147,16 @@ def tile_splatinformationflow_pb_kernel(
 
         def interleave_w_gpsimd(g, h):
             wg = wst.tile([P, NH, 4], BF16, name="wg", tag="wg", bufs=2, align_bytes=64)
-            nc.gpsimd.tensor_scalar(
-                out=wg[:], in0=wraw_t[(g, h)][:].rearrange("p j n -> p n j"), scalar1=1.0, scalar2=0.0, op0=MULT, op1=ADD
-            )
+            w = NH // WG_SPLIT
+            for s in range(WG_SPLIT):
+                nc.gpsimd.tensor_scalar(
+                    out=wg[:, s * w : (s + 1) * w, :],
+                    in0=wraw_t[(g, h)][:, :, s * w : (s + 1) * w].rearrange("p j n -> p n j"),
+                    scalar1=1.0,
+                    scalar2=0.0,
+                    op0=MULT,
+                    op1=ADD,
+                )
             wg_t[(g, h)] = wg
 
         def quantize_w(g, h):
@@ -151,15 +167,36 @@ def tile_splatinformationflow_pb_kernel(
                 in_=wg_t[(g, h)][:].rearrange("p n j -> p (n j)"),
             )
 
+        def sort_words(j):
+            for t in DEINT:
+                xd = xin.tile([P, 2, 2 * P, 2], BF16, name="xd", tag="xd", bufs=XD_BUFS)
+                nc.gpsimd.tensor_scalar(
+                    out=xd[:],
+                    in0=x_t[j][:, t, :].rearrange("p (w u e) -> p u w e", u=2, e=2),
+                    scalar1=1.0,
+                    scalar2=0.0,
+                    op0=MULT,
+                    op1=ADD,
+                )
+                xd_t[(j, t)] = xd
+
         def transpose_x(j):
             for t in range(2):
                 xt = psum.tile([P, 2, 2, P], F32, name="xt", tag="xt", bufs=XT_BUFS)
-                words = x_t[j][:, t, :].bitcast(F32)
-                for g in range(2):
-                    for u in range(2):
-                        nc.tensor.transpose(
-                            xt[:, g, u, :], words[:, 256 * g + u : 256 * (g + 1) : 2], ident_f[:]
-                        )
+                if (j, t) in xd_t:
+                    sorted_words = xd_t[(j, t)][:].rearrange("p u w e -> p (u w e)").bitcast(F32)
+                    for g in range(2):
+                        for u in range(2):
+                            nc.tensor.transpose(
+                                xt[:, g, u, :], sorted_words[:, 256 * u + P * g : 256 * u + P * (g + 1)], ident_f[:]
+                            )
+                else:
+                    words = x_t[j][:, t, :].bitcast(F32)
+                    for g in range(2):
+                        for u in range(2):
+                            nc.tensor.transpose(
+                                xt[:, g, u, :], words[:, 256 * g + u : 256 * (g + 1) : 2], ident_f[:]
+                            )
                 xt_t[(j, t)] = xt
 
         def regroup_x(j, t, engine):
@@ -242,7 +279,14 @@ def tile_splatinformationflow_pb_kernel(
             if offloaded(n - LAG_P):
                 fs = ep.tile([P, NH], F32, name="fs", tag="fs", bufs=FS_BUFS)
                 nc.scalar.copy(out=fs[:], in_=fl_t[u][:])
-                nc.gpsimd.tensor_tensor(out=dst, in0=zb_t[u][:], in1=fs[:], op=MULT)
+                w = NH // GP_SPLIT
+                for s in range(GP_SPLIT):
+                    nc.gpsimd.tensor_tensor(
+                        out=dst[:, s * w : (s + 1) * w],
+                        in0=zb_t[u][:, s * w : (s + 1) * w],
+                        in1=fs[:, s * w : (s + 1) * w],
+                        op=MULT,
+                    )
             else:
                 nc.vector.tensor_tensor(out=dst, in0=fl_t[u][:], in1=zb_t[u][:], op=MULT)
 
@@ -256,11 +300,10 @@ def tile_splatinformationflow_pb_kernel(
         load_x(1)
         nc.sync.dma_start(out=brow[0:1, :], in_=gate_b.rearrange("(o n) -> o n", o=1))
         load_batch(0)
-        load_x(2)
-        load_x(3)
-        load_w(0, 1)
-        load_w(1, 1)
-        for j in range(4, PREFETCH):
+        for j in range(2, PREFETCH):
+            if j == WL_BEFORE:
+                load_w(0, 1)
+                load_w(1, 1)
             load_x(j)
         load_batch(1)
 
@@ -303,6 +346,9 @@ def tile_splatinformationflow_pb_kernel(
                     load_x(j + PREFETCH)
                 if j % 4 == 0 and j // 4 + 2 < NB:
                     load_batch(j // 4 + 2)
+            for j in tr_at.get(n + DE_LEAD, []):
+                if j >= DE_FROM:
+                    sort_words(j)
             for j in tr_at.get(n, []):
                 transpose_x(j)
                 if j % 4 == 0:
@@ -318,6 +364,10 @@ def tile_splatinformationflow_pb_kernel(
                 flow_matmul(uf)
             if u is not None:
                 add_bias(u)
+            if QZ_MID:
+                for j in tr_at.get(n - QZ_DELAY, [])[:1]:
+                    if j >= 4:
+                        quantize_x(j)
             if up is not None:
                 product(up, n)
             if u is not None:
@@ -336,7 +386,7 @@ def tile_splatinformationflow_pb_kernel(
             for j in tr_at.get(n - QZ_HEAD, []):
                 if j < 4:
                     quantize_x(j)
-            for j in tr_at.get(n - QZ_DELAY, [])[:1]:
+            for j in tr_at.get(n - QZ_DELAY, [])[: (0 if QZ_MID else 1)]:
                 if j >= 4:
                     quantize_x(j)
             for j in tr_at.get(n - QZ_DELAY - 2, [])[1:]:

@@ -32,12 +32,12 @@ TAIL_FROM = 52
 HEAD_TR = (1, 3)
 SIT0_AT = 0
 WL_BEFORE = 4
-DEINT = ()
+DEINT = (1,)
 XD_BUFS = 4
 DE_FROM = 4
-DE_LEAD = 4
-GP_SPLIT = 4
-WG_SPLIT = 8
+DE_LEAD = 6
+GP_SPLIT = 1
+WG_SPLIT = 1
 QZ_MID = False
 CP_DELAY = (0, 0)
 QZ_DELAY = 3

@@ -3,79 +3,50 @@ from contextlib import ExitStack
 import concourse.masks as masks
 import concourse.mybir as mybir
 
-NB, S, D, KS = 4, 1024, 1024, 128
-FLOPS = 2 * NB * S * D * D + 2 * NB * S * KS * D
+BATCHES, TOKENS, FEATURES, SPLATS = 4, 1024, 1024, 128
+FLOPS = 2 * BATCHES * TOKENS * FEATURES * FEATURES + 2 * BATCHES * TOKENS * SPLATS * FEATURES
 
 F32 = mybir.dt.float32
 BF16 = mybir.dt.bfloat16
 U32 = mybir.dt.uint32
 U8 = mybir.dt.uint8
-E5X4 = mybir.dt.float8_e5m2_x4
+E5M2_X4 = mybir.dt.float8_e5m2_x4
 ADD = mybir.AluOpType.add
 MULT = mybir.AluOpType.mult
 SIGMOID = mybir.ActivationFunctionType.Sigmoid
 
 P = 128
-NH = 512
-TPB = S // P
-NTILES = NB * TPB
-NPER = NTILES // 2
-PREFETCH = 6
-LEAD = 2
-W_VEC_COLS = 336
-W_LATE = (4, 6)
-OFF_MOD = 8
-OFFLOAD = (1, 4, 6)
-OFF_HEAD = (1, 4, 6)
-OFF_TAIL = (0, 2, 4, 6)
-TAIL_FROM = 52
-HEAD_TR = (1, 3)
-SIT0_AT = 0
-WL_BEFORE = 4
-DEINT = (1,)
-XD_BUFS = 4
-DE_FROM = 4
-DE_LEAD = 6
-GP_SPLIT = 1
-WG_SPLIT = 1
-QZ_MID = False
-CP_DELAY = (0, 0)
-QZ_DELAY = 3
-LAG_F = 2
-LAG_P = 2
-ZB_BUFS = 6
-FS_BUFS = 2
-HM = 8
-OFF_LAST = 2
-O_BUFS = 10
-QZ_HEAD = 1
-XQ_BUFS = 6
-Z_BUFS = 3
-FL_BUFS = 3
-XT_BUFS = 2
-TR_PAIR = False
-CP_EARLY = True
-W_GP = True
-TR_SHIFT = 0
+PACK = 4
+K_PASS = P * PACK
+PASSES = FEATURES // K_PASS
+HALF = 512
+WORDS_PER_PASS = K_PASS // 2
+TILES_PER_BATCH = TOKENS // P
+TILES = BATCHES * TILES_PER_BATCH
+PERIODS = TILES // 2
+PERIODS_PER_BATCH = TILES_PER_BATCH // 2
+UNITS = 2 * TILES
+UNITS_PER_PERIOD = 4
+UNITS_PER_BATCH = 2 * TILES_PER_BATCH
 
-
-def offloaded(m):
-    if m < 16:
-        return m % 8 in OFF_HEAD
-    if m < TAIL_FROM:
-        return m % 8 in OFFLOAD
-    return m % 8 in OFF_TAIL and m < 2 * NTILES - OFF_LAST
+LOADS_AHEAD = 6
+PRODUCT_LAG = 2
+TILES_STORED_BY_HALVES = 2
+LAST_ON_VECTOR = 4
+TRANSPOSES_AHEAD = 2
+VECTOR_COLUMNS = 336
+LAST_TRANSPOSE_STEP = UNITS_PER_PERIOD * (PERIODS - 1 - TRANSPOSES_AHEAD)
 
 
 def unit_order():
-    units = []
-    for h in range(2):
-        for i in range(HM):
-            units.append((i, h))
-    for i in range(HM, NTILES):
-        for h in range(2):
-            units.append((i, h))
-    return units
+    first_batch = [(i, h) for h in range(2) for i in range(TILES_PER_BATCH)]
+    return first_batch + [(i, h) for i in range(TILES_PER_BATCH, TILES) for h in range(2)]
+
+
+def product_on_gpsimd(n):
+    if n < LAST_TRANSPOSE_STEP:
+        return n % 8 in (1, 4, 7)
+    return n % 2 == 0 and n < UNITS - LAST_ON_VECTOR
 
 
 def tile_splatinformationflow_pb_kernel(
@@ -84,312 +55,242 @@ def tile_splatinformationflow_pb_kernel(
     nc = tc.nc
     with ExitStack() as ctx:
         const = ctx.enter_context(tc.tile_pool(name="const", bufs=1))
-        xin = ctx.enter_context(tc.tile_pool(name="xin", bufs=NPER))
-        batch = ctx.enter_context(tc.tile_pool(name="batch", bufs=NB))
-        wst = ctx.enter_context(tc.tile_pool(name="wst", bufs=4))
-        xq = ctx.enter_context(tc.tile_pool(name="xq", bufs=XQ_BUFS))
-        ep = ctx.enter_context(tc.tile_pool(name="ep", bufs=4))
-        psum = ctx.enter_context(tc.psum_pool(name="psum", bufs=Z_BUFS))
+        tokens_in = ctx.enter_context(tc.tile_pool(name="tokens_in", bufs=PERIODS))
+        per_batch = ctx.enter_context(tc.tile_pool(name="per_batch", bufs=BATCHES))
+        weights_in = ctx.enter_context(tc.tile_pool(name="weights_in", bufs=2 * PASSES))
+        codes = ctx.enter_context(tc.tile_pool(name="codes", bufs=6))
+        epilogue = ctx.enter_context(tc.tile_pool(name="epilogue", bufs=6))
+        psum = ctx.enter_context(tc.psum_pool(name="psum", bufs=3))
         ctx.enter_context(tc.manual_schedule())
 
-        x_view = [token_embeddings[b].rearrange("(p c) k -> p c k", c=TPB) for b in range(NB)]
-        si_view = [splat_influences[b].rearrange("(p c) s -> p c s", c=TPB) for b in range(NB)]
-        out_view = [out[b].rearrange("(p c) n -> p c n", c=TPB) for b in range(NB)]
+        tokens_view = [token_embeddings[b].rearrange("(p c) k -> p c k", c=TILES_PER_BATCH) for b in range(BATCHES)]
+        influences_view = [splat_influences[b].rearrange("(p c) s -> p c s", c=TILES_PER_BATCH) for b in range(BATCHES)]
+        out_view = [out[b].rearrange("(p c) n -> p c n", c=TILES_PER_BATCH) for b in range(BATCHES)]
 
-        x_t, si_t, dec_t, sit_t, wraw_t = {}, {}, {}, {}, {}
-        xt_t, xg_t, xc_t, xs_t = {}, {}, {}, {}
-        z_t, fl_t, zb_t, o_t = {}, {}, {}, {}
-        wg_t = {}
-        xd_t = {}
+        tokens, influences, influences_t, states = {}, {}, {}, {}
+        weights_raw, weights_grouped = {}, {}
+        words_t, tokens_grouped, token_codes, token_scales = {}, {}, {}, {}
+        z_banks, flow_banks, gates, results = {}, {}, {}, {}
 
         warm = const.tile([P, 1], F32, name="warm")
         nc.vector.memset(warm[:], 0.0)
         nc.scalar.activation(out=warm[:], in_=warm[:], func=SIGMOID)
-        ident_f = const.tile([P, P], F32, name="ident_f")
-        masks.make_identity(nc, ident_f[:])
-        ident_b = const.tile([P, P], BF16, name="ident_b")
-        masks.make_identity(nc, ident_b[:])
+        identity_f32 = const.tile([P, P], F32, name="identity_f32")
+        masks.make_identity(nc, identity_f32[:])
+        identity_bf16 = const.tile([P, P], BF16, name="identity_bf16")
+        masks.make_identity(nc, identity_bf16[:])
         ones = const.tile([P, P], BF16, name="ones")
         nc.vector.memset(ones[:], 1.0)
-        brow = const.tile([P, D], BF16, name="brow")
-        nc.vector.memset(brow[:], 0.0)
-        bias_sb = const.tile([P, D], F32, name="bias_sb")
-        wc = const.tile([P, 2, D], U32, name="wc", align_bytes=64)
-        ws = const.tile([P, 2, D], U8, name="ws", align_bytes=64)
+        bias_row = const.tile([P, FEATURES], BF16, name="bias_row")
+        nc.vector.memset(bias_row[:], 0.0)
+        bias = const.tile([P, FEATURES], F32, name="bias")
+        weight_codes = const.tile([P, PASSES, FEATURES], U32, name="weight_codes", align_bytes=64)
+        weight_scales = const.tile([P, PASSES, FEATURES], U8, name="weight_scales", align_bytes=64)
 
-        def load_x(j):
-            x = xin.tile([P, 2, D], BF16, name="x", tag="x")
-            b, c = (2 * j) // TPB, (2 * j) % TPB
-            nc.sync.dma_start(out=x[:], in_=x_view[b][:, c : c + 2, :])
-            x_t[j] = x
+        def half_columns(h):
+            return slice(HALF * h, HALF * (h + 1))
 
-        def load_w(g, h):
-            wraw = wst.tile([P, 4, NH], BF16, name="wraw", tag="wraw")
-            rows = gate_W[512 * g : 512 * (g + 1), NH * h : NH * (h + 1)]
-            nc.sync.dma_start(out=wraw[:], in_=rows.rearrange("(p j) n -> p j n", j=4))
-            wraw_t[(g, h)] = wraw
+        def load_tokens(j):
+            b, c = (2 * j) // TILES_PER_BATCH, (2 * j) % TILES_PER_BATCH
+            raw = tokens_in.tile([P, 2, FEATURES], BF16, name="tokens", tag="tokens")
+            nc.sync.dma_start(out=raw[:], in_=tokens_view[b][:, c : c + 2, :])
+            tokens[j] = raw
+
+        def load_weights(g, h):
+            raw = weights_in.tile([P, PACK, HALF], BF16, name="weights_raw", tag="weights_raw")
+            rows = gate_W[K_PASS * g : K_PASS * (g + 1), half_columns(h)]
+            nc.sync.dma_start(out=raw[:], in_=rows.rearrange("(p j) n -> p j n", j=PACK))
+            weights_raw[(g, h)] = raw
 
         def load_batch(b):
-            si = batch.tile([P, TPB, KS], BF16, name="si", tag="si")
-            nc.sync.dma_start(out=si[:], in_=si_view[b])
-            si_t[b] = si
-            dec = batch.tile([P, D], BF16, name="dec", tag="dec")
-            nc.sync.dma_start(out=dec[:], in_=decoded[b])
-            dec_t[b] = dec
+            raw = per_batch.tile([P, TILES_PER_BATCH, SPLATS], BF16, name="influences", tag="influences")
+            nc.sync.dma_start(out=raw[:], in_=influences_view[b])
+            influences[b] = raw
+            state = per_batch.tile([P, FEATURES], BF16, name="states", tag="states")
+            nc.sync.dma_start(out=state[:], in_=decoded[b])
+            states[b] = state
 
-        def interleave_w(g, h):
-            wraw = wraw_t[(g, h)]
-            wg = wst.tile([P, NH, 4], BF16, name="wg", tag="wg", bufs=2, align_bytes=64)
-            v = W_VEC_COLS
-            nc.vector.tensor_copy(out=wg[:, :v, :], in_=wraw[:, :, :v].rearrange("p j n -> p n j"))
-            nc.scalar.copy(out=wg[:, v:, :], in_=wraw[:, :, v:].rearrange("p j n -> p n j"))
-            wg_t[(g, h)] = wg
+        def interleave_weights(g, h):
+            raw = weights_raw[(g, h)]
+            grouped = weights_in.tile([P, HALF, PACK], BF16, name="weights_grouped", tag="weights_grouped", bufs=2, align_bytes=64)
+            v = VECTOR_COLUMNS
+            nc.vector.tensor_copy(out=grouped[:, :v, :], in_=raw[:, :, :v].rearrange("p j n -> p n j"))
+            nc.scalar.copy(out=grouped[:, v:, :], in_=raw[:, :, v:].rearrange("p j n -> p n j"))
+            weights_grouped[(g, h)] = grouped
 
-        def interleave_w_gpsimd(g, h):
-            wg = wst.tile([P, NH, 4], BF16, name="wg", tag="wg", bufs=2, align_bytes=64)
-            w = NH // WG_SPLIT
-            for s in range(WG_SPLIT):
-                nc.gpsimd.tensor_scalar(
-                    out=wg[:, s * w : (s + 1) * w, :],
-                    in0=wraw_t[(g, h)][:, :, s * w : (s + 1) * w].rearrange("p j n -> p n j"),
-                    scalar1=1.0,
-                    scalar2=0.0,
-                    op0=MULT,
-                    op1=ADD,
-                )
-            wg_t[(g, h)] = wg
-
-        def quantize_w(g, h):
-            hs = slice(NH * h, NH * (h + 1))
+        def quantize_weights(g, h):
             nc.vector.quantize_mx(
-                out=wc[:, g, hs].bitcast(E5X4),
-                scales=ws[:, g, hs],
-                in_=wg_t[(g, h)][:].rearrange("p n j -> p (n j)"),
+                out=weight_codes[:, g, half_columns(h)].bitcast(E5M2_X4),
+                scales=weight_scales[:, g, half_columns(h)],
+                in_=weights_grouped[(g, h)][:].rearrange("p n j -> p (n j)"),
             )
 
-        def sort_words(j):
-            for t in DEINT:
-                xd = xin.tile([P, 2, 2 * P, 2], BF16, name="xd", tag="xd", bufs=XD_BUFS)
-                nc.gpsimd.tensor_scalar(
-                    out=xd[:],
-                    in0=x_t[j][:, t, :].rearrange("p (w u e) -> p u w e", u=2, e=2),
-                    scalar1=1.0,
-                    scalar2=0.0,
-                    op0=MULT,
-                    op1=ADD,
-                )
-                xd_t[(j, t)] = xd
-
-        def transpose_x(j):
+        def transpose_tokens(j):
             for t in range(2):
-                xt = psum.tile([P, 2, 2, P], F32, name="xt", tag="xt", bufs=XT_BUFS)
-                if (j, t) in xd_t:
-                    sorted_words = xd_t[(j, t)][:].rearrange("p u w e -> p (u w e)").bitcast(F32)
-                    for g in range(2):
-                        for u in range(2):
-                            nc.tensor.transpose(
-                                xt[:, g, u, :], sorted_words[:, 256 * u + P * g : 256 * u + P * (g + 1)], ident_f[:]
-                            )
-                else:
-                    words = x_t[j][:, t, :].bitcast(F32)
-                    for g in range(2):
-                        for u in range(2):
-                            nc.tensor.transpose(
-                                xt[:, g, u, :], words[:, 256 * g + u : 256 * (g + 1) : 2], ident_f[:]
-                            )
-                xt_t[(j, t)] = xt
+                bank = psum.tile([P, PASSES, 2, P], F32, name="words_t", tag="words_t", bufs=2)
+                words = tokens[j][:, t, :].bitcast(F32)
+                for g in range(PASSES):
+                    for u in range(2):
+                        nc.tensor.transpose(bank[:, g, u, :], words[:, WORDS_PER_PASS * g + u : WORDS_PER_PASS * (g + 1) : 2], identity_f32[:])
+                words_t[(j, t)] = bank
 
-        def regroup_x(j, t, engine):
+        def regroup_tokens(j, t, copy):
             if t == 0:
-                xg_new = xq.tile([P, 2, D], BF16, name="xg", tag="xg", bufs=3, align_bytes=64)
-                xg_t[j] = xg_new
-            dst = xg_t[j][:, t, :].bitcast(F32).rearrange("p (g r u) -> p g r u", g=2, u=2)
-            src = xt_t[(j, t)][:].rearrange("p g u r -> p g r u")
-            if engine == "v":
-                nc.vector.tensor_copy(out=dst, in_=src)
-            else:
-                nc.scalar.copy(out=dst, in_=src)
-
-        def quantize_x(j):
-            xc = xq.tile([P, 4 * P], U32, name="xc", tag="xc", align_bytes=64)
-            xs = xq.tile([P, 4 * P], U8, name="xs", tag="xs", align_bytes=64)
-            nc.vector.quantize_mx(
-                out=xc[:].bitcast(E5X4), scales=xs[:], in_=xg_t[j][:].rearrange("p t c -> p (t c)")
+                fresh = codes.tile([P, 2, FEATURES], BF16, name="tokens_grouped", tag="tokens_grouped", bufs=3, align_bytes=64)
+                tokens_grouped[j] = fresh
+            copy(
+                out=tokens_grouped[j][:, t, :].bitcast(F32).rearrange("p (g r u) -> p g r u", g=PASSES, u=2),
+                in_=words_t[(j, t)][:].rearrange("p g u r -> p g r u"),
             )
-            xc_t[j] = xc
-            xs_t[j] = xs
 
-        def transpose_si(b):
-            sp = psum.tile([P, TPB, P], BF16, name="sp", tag="fl", bufs=FL_BUFS)
-            for c in range(TPB):
-                nc.tensor.transpose(sp[:, c, :], si_t[b][:, c, :], ident_b[:])
-            sit = batch.tile([P, TPB, P], BF16, name="sit", tag="sit")
-            nc.scalar.copy(out=sit[:], in_=sp[:])
-            sit_t[b] = sit
+        def quantize_tokens(j):
+            packed = codes.tile([P, 2 * PASSES * P], U32, name="token_codes", tag="token_codes", align_bytes=64)
+            scale_bytes = codes.tile([P, 2 * PASSES * P], U8, name="token_scales", tag="token_scales", align_bytes=64)
+            nc.vector.quantize_mx(
+                out=packed[:].bitcast(E5M2_X4), scales=scale_bytes[:], in_=tokens_grouped[j][:].rearrange("p t c -> p (t c)")
+            )
+            token_codes[j] = packed
+            token_scales[j] = scale_bytes
+
+        def transpose_influences(b):
+            bank = psum.tile([P, TILES_PER_BATCH, P], BF16, name="influences_bank", tag="flow")
+            for c in range(TILES_PER_BATCH):
+                nc.tensor.transpose(bank[:, c, :], influences[b][:, c, :], identity_bf16[:])
+            turned = per_batch.tile([P, TILES_PER_BATCH, P], BF16, name="influences_t", tag="influences_t")
+            nc.scalar.copy(out=turned[:], in_=bank[:])
+            influences_t[b] = turned
 
         def spread_bias():
             for h in range(2):
-                hs = slice(NH * h, NH * (h + 1))
-                bp = psum.tile([P, NH], F32, name="bp", tag="z")
-                nc.tensor.matmul(out=bp[:], lhsT=ones[:], rhs=brow[:, hs], start=True, stop=True)
-                nc.scalar.copy(out=bias_sb[:, hs], in_=bp[:])
+                bank = psum.tile([P, HALF], F32, name="bias_bank", tag="z")
+                nc.tensor.matmul(out=bank[:], lhsT=ones[:], rhs=bias_row[:, half_columns(h)], start=True, stop=True)
+                nc.scalar.copy(out=bias[:, half_columns(h)], in_=bank[:])
 
-        def gate_matmul(u):
-            i, h = u
+        def gate_matmul(unit):
+            i, h = unit
             j, t = i // 2, i % 2
-            hs = slice(NH * h, NH * (h + 1))
-            z = psum.tile([P, NH], F32, name="z", tag="z")
-            for g in range(2):
-                cols = slice((2 * t + g) * P, (2 * t + g + 1) * P)
+            bank = psum.tile([P, HALF], F32, name="z", tag="z")
+            for g in range(PASSES):
+                token_columns = slice((PASSES * t + g) * P, (PASSES * t + g + 1) * P)
                 nc.tensor.matmul_mx(
-                    out=z[:],
-                    lhsT=xc_t[j][:, cols].bitcast(E5X4),
-                    lhsT_scale=xs_t[j][:, cols],
-                    rhs=wc[:, g, hs].bitcast(E5X4),
-                    rhs_scale=ws[:, g, hs],
+                    out=bank[:],
+                    lhsT=token_codes[j][:, token_columns].bitcast(E5M2_X4),
+                    lhsT_scale=token_scales[j][:, token_columns],
+                    rhs=weight_codes[:, g, half_columns(h)].bitcast(E5M2_X4),
+                    rhs_scale=weight_scales[:, g, half_columns(h)],
                     start=(g == 0),
-                    stop=(g == 1),
+                    stop=(g == PASSES - 1),
                 )
-            z_t[u] = z
+            z_banks[unit] = bank
 
-        def flow_matmul(u):
-            i, h = u
-            b, c = i // TPB, i % TPB
-            fl = psum.tile([P, NH], F32, name="fl", tag="fl", bufs=FL_BUFS)
-            nc.tensor.matmul(
-                out=fl[:], lhsT=sit_t[b][:, c, :], rhs=dec_t[b][:, NH * h : NH * (h + 1)], start=True, stop=True
-            )
-            fl_t[u] = fl
+        def flow_matmul(unit):
+            i, h = unit
+            b, c = i // TILES_PER_BATCH, i % TILES_PER_BATCH
+            bank = psum.tile([P, HALF], F32, name="flow", tag="flow")
+            nc.tensor.matmul(out=bank[:], lhsT=influences_t[b][:, c, :], rhs=states[b][:, half_columns(h)], start=True, stop=True)
+            flow_banks[unit] = bank
 
-        def add_bias(u):
-            h = u[1]
-            zb = ep.tile([P, NH], F32, name="zb", tag="zb", bufs=ZB_BUFS)
-            nc.vector.tensor_tensor(out=zb[:], in0=z_t[u][:], in1=bias_sb[:, NH * h : NH * (h + 1)], op=ADD)
-            zb_t[u] = zb
+        def add_bias(unit):
+            gate = epilogue.tile([P, HALF], F32, name="gate", tag="gate")
+            nc.vector.tensor_tensor(out=gate[:], in0=z_banks[unit][:], in1=bias[:, half_columns(unit[1])], op=ADD)
+            gates[unit] = gate
 
-        def sigmoid(u):
-            nc.scalar.activation(out=zb_t[u][:], in_=zb_t[u][:], func=SIGMOID)
+        def sigmoid(unit):
+            nc.scalar.activation(out=gates[unit][:], in_=gates[unit][:], func=SIGMOID)
 
-        def product(u, n):
-            i, h = u
-            if i not in o_t:
-                o_new = ep.tile([P, D], F32, name="o", tag="o", bufs=O_BUFS)
-                o_t[i] = o_new
-            dst = o_t[i][:, NH * h : NH * (h + 1)]
-            if offloaded(n - LAG_P):
-                fs = ep.tile([P, NH], F32, name="fs", tag="fs", bufs=FS_BUFS)
-                nc.scalar.copy(out=fs[:], in_=fl_t[u][:])
-                w = NH // GP_SPLIT
-                for s in range(GP_SPLIT):
-                    nc.gpsimd.tensor_tensor(
-                        out=dst[:, s * w : (s + 1) * w],
-                        in0=zb_t[u][:, s * w : (s + 1) * w],
-                        in1=fs[:, s * w : (s + 1) * w],
-                        op=MULT,
-                    )
+        def product(unit, on_gpsimd):
+            i, h = unit
+            if i not in results:
+                fresh = epilogue.tile([P, FEATURES], F32, name="result", tag="result", bufs=10)
+                results[i] = fresh
+            target = results[i][:, half_columns(h)]
+            if on_gpsimd:
+                flow = epilogue.tile([P, HALF], F32, name="flow_copy", tag="flow_copy", bufs=2)
+                nc.scalar.copy(out=flow[:], in_=flow_banks[unit][:])
+                nc.gpsimd.tensor_tensor(out=target, in0=gates[unit][:], in1=flow[:], op=MULT)
             else:
-                nc.vector.tensor_tensor(out=dst, in0=fl_t[u][:], in1=zb_t[u][:], op=MULT)
+                nc.vector.tensor_tensor(out=target, in0=flow_banks[unit][:], in1=gates[unit][:], op=MULT)
 
-        def store(i):
-            b, c = i // TPB, i % TPB
-            nc.sync.dma_start(out=out_view[b][:, c, :], in_=o_t[i][:])
+        def store(i, columns):
+            b, c = i // TILES_PER_BATCH, i % TILES_PER_BATCH
+            nc.sync.dma_start(out=out_view[b][:, c, columns], in_=results[i][:, columns])
 
-        load_x(0)
-        load_w(0, 0)
-        load_w(1, 0)
-        load_x(1)
-        nc.sync.dma_start(out=brow[0:1, :], in_=gate_b.rearrange("(o n) -> o n", o=1))
+        load_tokens(0)
+        load_weights(0, 0)
+        load_weights(1, 0)
+        load_tokens(1)
+        nc.sync.dma_start(out=bias_row[0:1, :], in_=gate_b.rearrange("(o n) -> o n", o=1))
         load_batch(0)
-        for j in range(2, PREFETCH):
-            if j == WL_BEFORE:
-                load_w(0, 1)
-                load_w(1, 1)
-            load_x(j)
+        load_tokens(2)
+        load_tokens(3)
+        load_weights(0, 1)
+        load_weights(1, 1)
+        load_tokens(4)
+        load_tokens(5)
         load_batch(1)
 
-        transpose_x(0)
-        regroup_x(0, 0, "v")
-        regroup_x(0, 1, "s")
-        interleave_w(0, 0)
-        interleave_w(1, 0)
-        quantize_w(0, 0)
-        quantize_x(0)
-        quantize_w(1, 0)
-        transpose_x(1)
-        regroup_x(1, 0, "s")
-        regroup_x(1, 1, "s")
+        transpose_tokens(0)
+        regroup_tokens(0, 0, nc.vector.tensor_copy)
+        regroup_tokens(0, 1, nc.scalar.copy)
+        interleave_weights(0, 0)
+        interleave_weights(1, 0)
+        quantize_weights(0, 0)
+        quantize_tokens(0)
+        quantize_weights(1, 0)
+        transpose_tokens(1)
+        regroup_tokens(1, 0, nc.scalar.copy)
+        regroup_tokens(1, 1, nc.scalar.copy)
         spread_bias()
-        quantize_x(1)
-
-        if W_GP:
-            interleave_w_gpsimd(0, 1)
-            interleave_w_gpsimd(1, 1)
+        quantize_tokens(1)
 
         units = unit_order()
-        tr_at = {}
-        for j in range(2, NPER):
-            if j - 2 < len(HEAD_TR):
-                tr_at[HEAD_TR[j - 2]] = [j]
-            elif TR_PAIR:
-                tr_at.setdefault(8 * ((j - LEAD) // 2) - TR_SHIFT, []).append(j)
-            else:
-                tr_at[4 * (j - LEAD)] = [j]
-        late = {W_LATE[0]: (0, 1), W_LATE[1]: (1, 1)}
-        done_halves = {}
-        for n in range(len(units) + LAG_P):
-            u = units[n] if n < len(units) else None
-            uf = units[n - LAG_F] if 0 <= n - LAG_F < len(units) else None
-            up = units[n - LAG_P] if n >= LAG_P else None
-            if n % 4 == 0:
-                j = n // 4
-                if j + PREFETCH < NPER:
-                    load_x(j + PREFETCH)
-                if j % 4 == 0 and j // 4 + 2 < NB:
-                    load_batch(j // 4 + 2)
-            for j in tr_at.get(n + DE_LEAD, []):
-                if j >= DE_FROM:
-                    sort_words(j)
-            for j in tr_at.get(n, []):
-                transpose_x(j)
-                if j % 4 == 0:
-                    transpose_si(j // 4)
-                if CP_EARLY:
-                    regroup_x(j, 0, "s")
-                    regroup_x(j, 1, "s")
-            if u is not None:
-                gate_matmul(u)
-                if n == SIT0_AT:
-                    transpose_si(0)
-            if uf is not None:
-                flow_matmul(uf)
-            if u is not None:
-                add_bias(u)
-            if QZ_MID:
-                for j in tr_at.get(n - QZ_DELAY, [])[:1]:
-                    if j >= 4:
-                        quantize_x(j)
-            if up is not None:
-                product(up, n)
-            if u is not None:
-                sigmoid(u)
-            for j in tr_at.get(n - CP_DELAY[0], [])[: (0 if CP_EARLY else 1)]:
-                regroup_x(j, 0, "s")
-                regroup_x(j, 1, "s")
-            for j in tr_at.get(n - CP_DELAY[1], [])[1:]:
-                regroup_x(j, 0, "s")
-                regroup_x(j, 1, "s")
-            if up is not None:
-                i = up[0]
-                done_halves[i] = done_halves.get(i, 0) + 1
-                if done_halves[i] == 2:
-                    store(i)
-            for j in tr_at.get(n - QZ_HEAD, []):
-                if j < 4:
-                    quantize_x(j)
-            for j in tr_at.get(n - QZ_DELAY, [])[: (0 if QZ_MID else 1)]:
-                if j >= 4:
-                    quantize_x(j)
-            for j in tr_at.get(n - QZ_DELAY - 2, [])[1:]:
-                quantize_x(j)
-            if n in late:
-                quantize_w(late[n][0], late[n][1])
+        transposed_at = {}
+        for j in range(2, PERIODS):
+            transposed_at[2 * j - 3 if j < PERIODS_PER_BATCH else UNITS_PER_PERIOD * (j - TRANSPOSES_AHEAD)] = j
+        right_half_at = {3: 0, 5: 1}
+        halves_done = {}
+
+        for n in range(UNITS + PRODUCT_LAG):
+            unit = units[n] if n < UNITS else None
+            behind = units[n - PRODUCT_LAG] if n >= PRODUCT_LAG else None
+
+            if n % UNITS_PER_PERIOD == 0 and n // UNITS_PER_PERIOD + LOADS_AHEAD < PERIODS:
+                load_tokens(n // UNITS_PER_PERIOD + LOADS_AHEAD)
+            if n % UNITS_PER_BATCH == 0 and n // UNITS_PER_BATCH + 2 < BATCHES:
+                load_batch(n // UNITS_PER_BATCH + 2)
+
+            if n in transposed_at:
+                j = transposed_at[n]
+                transpose_tokens(j)
+                if j % PERIODS_PER_BATCH == 0:
+                    transpose_influences(j // PERIODS_PER_BATCH)
+                regroup_tokens(j, 0, nc.scalar.copy)
+                regroup_tokens(j, 1, nc.scalar.copy)
+
+            if unit is not None:
+                gate_matmul(unit)
+                if n == 0:
+                    transpose_influences(0)
+            if behind is not None:
+                flow_matmul(behind)
+            if unit is not None:
+                add_bias(unit)
+            if transposed_at.get(n - 2, 0) >= PERIODS_PER_BATCH:
+                quantize_tokens(transposed_at[n - 2])
+            if behind is not None:
+                product(behind, product_on_gpsimd(n - PRODUCT_LAG))
+            if unit is not None:
+                sigmoid(unit)
+            if behind is not None:
+                i, h = behind
+                halves_done[i] = halves_done.get(i, 0) + 1
+                if i >= TILES - TILES_STORED_BY_HALVES:
+                    store(i, half_columns(h))
+                elif halves_done[i] == 2:
+                    store(i, slice(0, FEATURES))
+            if 0 < transposed_at.get(n - 1, 0) < PERIODS_PER_BATCH:
+                quantize_tokens(transposed_at[n - 1])
+            if n in right_half_at:
+                interleave_weights(right_half_at[n], 1)
+            if n - 1 in right_half_at:
+                quantize_weights(right_half_at[n - 1], 1)

@@ -29,7 +29,6 @@ UNITS = 2 * TILES
 UNITS_PER_PERIOD = 4
 UNITS_PER_BATCH = 2 * TILES_PER_BATCH
 
-LOADS_AHEAD = 6
 PRODUCT_LAG = 2
 TILES_STORED_BY_HALVES = 2
 LAST_ON_VECTOR = 4
@@ -228,6 +227,10 @@ def tile_splatinformationflow_pb_kernel(
         load_tokens(4)
         load_tokens(5)
         load_batch(1)
+        for j in range(6, PERIODS):
+            if j % PERIODS_PER_BATCH == 0:
+                load_batch(j // PERIODS_PER_BATCH)
+            load_tokens(j)
 
         transpose_tokens(0)
         regroup_tokens(0, 0, nc.vector.tensor_copy)
@@ -253,11 +256,6 @@ def tile_splatinformationflow_pb_kernel(
         for n in range(UNITS + PRODUCT_LAG):
             unit = units[n] if n < UNITS else None
             behind = units[n - PRODUCT_LAG] if n >= PRODUCT_LAG else None
-
-            if n % UNITS_PER_PERIOD == 0 and n // UNITS_PER_PERIOD + LOADS_AHEAD < PERIODS:
-                load_tokens(n // UNITS_PER_PERIOD + LOADS_AHEAD)
-            if n % UNITS_PER_BATCH == 0 and n // UNITS_PER_BATCH + 2 < BATCHES:
-                load_batch(n // UNITS_PER_BATCH + 2)
 
             if n in transposed_at:
                 j = transposed_at[n]

@@ -113,8 +113,12 @@ def tile_splatinformationflow_pb_kernel(
             raw = weights_raw[(g, h)]
             grouped = weights_in.tile([P, HALF, PACK], BF16, name="weights_grouped", tag="weights_grouped", bufs=2, align_bytes=64)
             v = VECTOR_COLUMNS
-            nc.vector.tensor_copy(out=grouped[:, :v, :], in_=raw[:, :, :v].rearrange("p j n -> p n j"))
-            nc.scalar.copy(out=grouped[:, v:, :], in_=raw[:, :, v:].rearrange("p j n -> p n j"))
+            nc.vector.tensor_copy(
+                out=grouped[:, :v, :].rearrange("p (c i) j -> p c j i", i=4), in_=raw[:, :, :v].rearrange("p j (c i) -> p c j i", i=4)
+            )
+            nc.scalar.copy(
+                out=grouped[:, v:, :].rearrange("p (c i) j -> p c j i", i=4), in_=raw[:, :, v:].rearrange("p j (c i) -> p c j i", i=4)
+            )
             weights_grouped[(g, h)] = grouped
 
         def quantize_weights(g, h):

@@ -85,6 +85,10 @@ def tile_splatinformationflow_pb_kernel(
         bias = const.tile([P, FEATURES], F32, name="bias")
         weight_codes = const.tile([P, PASSES, FEATURES], U32, name="weight_codes", align_bytes=64)
         weight_scales = const.tile([P, PASSES, FEATURES], U8, name="weight_scales", align_bytes=64)
+        turnstile = const.tile([P, 1], U32, name="turnstile")
+
+        def gpsimd_waits_for(code_words):
+            nc.gpsimd.tensor_copy(out=turnstile[:], in_=code_words)
 
         def half_columns(h):
             return slice(HALF * h, HALF * (h + 1))
@@ -127,6 +131,7 @@ def tile_splatinformationflow_pb_kernel(
                 scales=weight_scales[:, g, half_columns(h)],
                 in_=weights_grouped[(g, h)][:].rearrange("p n j -> p (n j)"),
             )
+            gpsimd_waits_for(weight_codes[:, g, HALF * h : HALF * h + 1])
 
         def transpose_tokens(j):
             for t in range(2):
@@ -152,6 +157,7 @@ def tile_splatinformationflow_pb_kernel(
             nc.vector.quantize_mx(
                 out=packed[:].bitcast(E5M2_X4), scales=scale_bytes[:], in_=tokens_grouped[j][:].rearrange("p t c -> p (t c)")
             )
+            gpsimd_waits_for(packed[:, 0:1])
             token_codes[j] = packed
             token_scales[j] = scale_bytes
 

@@ -58,7 +58,7 @@ def tile_splatinformationflow_pb_kernel(
         per_batch = ctx.enter_context(tc.tile_pool(name="per_batch", bufs=BATCHES))
         weights_in = ctx.enter_context(tc.tile_pool(name="weights_in", bufs=2 * PASSES))
         codes = ctx.enter_context(tc.tile_pool(name="codes", bufs=6))
-        epilogue = ctx.enter_context(tc.tile_pool(name="epilogue", bufs=6))
+        epilogue = ctx.enter_context(tc.tile_pool(name="epilogue", bufs=8))
         psum = ctx.enter_context(tc.psum_pool(name="psum", bufs=3))
         ctx.enter_context(tc.manual_schedule())
 
@@ -70,6 +70,8 @@ def tile_splatinformationflow_pb_kernel(
         weights_raw, weights_grouped = {}, {}
         words_t, tokens_grouped, token_codes, token_scales = {}, {}, {}, {}
         z_banks, flow_banks, gates, results = {}, {}, {}, {}
+        held_products = []
+        halves_done = {}
 
         warm = const.tile([P, 1], F32, name="warm")
         nc.vector.memset(warm[:], 0.0)
@@ -123,6 +125,7 @@ def tile_splatinformationflow_pb_kernel(
             nc.scalar.copy(
                 out=grouped[:, v:, :].rearrange("p (c i) j -> p c j i", i=4), in_=raw[:, :, v:].rearrange("p j (c i) -> p c j i", i=4)
             )
+            gpsimd_waits_for(grouped[:, 0, 0:2].bitcast(U32))
             weights_grouped[(g, h)] = grouped
 
         def quantize_weights(g, h):
@@ -214,15 +217,30 @@ def tile_splatinformationflow_pb_kernel(
                 results[i] = fresh
             target = results[i][:, half_columns(h)]
             if on_gpsimd:
-                flow = epilogue.tile([P, HALF], F32, name="flow_copy", tag="flow_copy", bufs=2)
+                flow = epilogue.tile([P, HALF], F32, name="flow_copy", tag="flow_copy", bufs=3)
                 nc.scalar.copy(out=flow[:], in_=flow_banks[unit][:])
-                nc.gpsimd.tensor_tensor(out=target, in0=gates[unit][:], in1=flow[:], op=MULT)
+                held_products.append((unit, target, gates[unit], flow))
             else:
                 nc.vector.tensor_tensor(out=target, in0=flow_banks[unit][:], in1=gates[unit][:], op=MULT)
+                store_what_is_whole(unit)
+
+        def release_products():
+            for unit, target, gate, flow in held_products:
+                nc.gpsimd.tensor_tensor(out=target, in0=gate[:], in1=flow[:], op=MULT)
+                store_what_is_whole(unit)
+            held_products.clear()
 
         def store(i, columns):
             b, c = i // TILES_PER_BATCH, i % TILES_PER_BATCH
             nc.sync.dma_start(out=out_view[b][:, c, columns], in_=results[i][:, columns])
+
+        def store_what_is_whole(unit):
+            i, h = unit
+            halves_done[i] = halves_done.get(i, 0) + 1
+            if i >= TILES - TILES_STORED_BY_HALVES:
+                store(i, half_columns(h))
+            elif halves_done[i] == 2:
+                store(i, slice(0, FEATURES))
 
         load_tokens(0)
         load_weights(0, 0)
@@ -261,7 +279,7 @@ def tile_splatinformationflow_pb_kernel(
         for j in range(2, PERIODS):
             transposed_at[2 * j - 3 if j < PERIODS_PER_BATCH else UNITS_PER_PERIOD * (j - TRANSPOSES_AHEAD)] = j
         right_half_at = {3: 0, 5: 1}
-        halves_done = {}
+        last_weight_step = max(right_half_at) + 1
 
         for n in range(UNITS + PRODUCT_LAG):
             unit = units[n] if n < UNITS else None
@@ -287,18 +305,15 @@ def tile_splatinformationflow_pb_kernel(
                 quantize_tokens(transposed_at[n - 2])
             if behind is not None:
                 product(behind, product_on_gpsimd(n - PRODUCT_LAG))
+            if n > last_weight_step and transposed_at.get(n - 1, 0) < PERIODS_PER_BATCH:
+                release_products()
             if unit is not None:
                 sigmoid(unit)
-            if behind is not None:
-                i, h = behind
-                halves_done[i] = halves_done.get(i, 0) + 1
-                if i >= TILES - TILES_STORED_BY_HALVES:
-                    store(i, half_columns(h))
-                elif halves_done[i] == 2:
-                    store(i, slice(0, FEATURES))
             if 0 < transposed_at.get(n - 1, 0) < PERIODS_PER_BATCH:
                 quantize_tokens(transposed_at[n - 1])
             if n in right_half_at:
                 interleave_weights(right_half_at[n], 1)
             if n - 1 in right_half_at:
                 quantize_weights(right_half_at[n - 1], 1)
+            if n == last_weight_step:
+                release_products()

@@ -43,6 +43,8 @@ def unit_order():
 
 
 def product_on_gpsimd(n):
+    if n < TILES_PER_BATCH:
+        return n in (0, 2, 4)
     if n < LAST_TRANSPOSE_STEP:
         return n % 8 in (1, 4, 7)
     return n % 2 == 0 and n < UNITS - LAST_ON_VECTOR
@@ -278,13 +280,18 @@ def tile_splatinformationflow_pb_kernel(
         transposed_at = {}
         for j in range(2, PERIODS):
             transposed_at[2 * j - 3 if j < PERIODS_PER_BATCH else UNITS_PER_PERIOD * (j - TRANSPOSES_AHEAD)] = j
-        right_half_at = {3: 0, 5: 1}
+        right_half_at = {1: 0, 4: 1}
         last_weight_step = max(right_half_at) + 1
 
         for n in range(UNITS + PRODUCT_LAG):
             unit = units[n] if n < UNITS else None
             behind = units[n - PRODUCT_LAG] if n >= PRODUCT_LAG else None
 
+            passes_first = n < TILES_PER_BATCH
+            if passes_first:
+                gate_matmul(unit)
+                if n == 0:
+                    transpose_influences(0)
             if n in transposed_at:
                 j = transposed_at[n]
                 transpose_tokens(j)
@@ -293,10 +300,8 @@ def tile_splatinformationflow_pb_kernel(
                 regroup_tokens(j, 0, nc.scalar.copy)
                 regroup_tokens(j, 1, nc.scalar.copy)
 
-            if unit is not None:
+            if unit is not None and not passes_first:
                 gate_matmul(unit)
-                if n == 0:
-                    transpose_influences(0)
             if behind is not None:
                 flow_matmul(behind)
             if unit is not None:

from contextlib import ExitStack

import concourse.masks as masks
import concourse.mybir as mybir

BATCHES, TOKENS, FEATURES, SPLATS = 4, 1024, 1024, 128
FLOPS = 2 * BATCHES * TOKENS * FEATURES * FEATURES + 2 * BATCHES * TOKENS * SPLATS * FEATURES

F32 = mybir.dt.float32
BF16 = mybir.dt.bfloat16
U32 = mybir.dt.uint32
U8 = mybir.dt.uint8
E5M2_X4 = mybir.dt.float8_e5m2_x4
ADD = mybir.AluOpType.add
MULT = mybir.AluOpType.mult
SIGMOID = mybir.ActivationFunctionType.Sigmoid

P = 128
PACK = 4
K_PASS = P * PACK
PASSES = FEATURES // K_PASS
HALF = 512
WORDS_PER_PASS = K_PASS // 2
TILES_PER_BATCH = TOKENS // P
TILES = BATCHES * TILES_PER_BATCH
PERIODS = TILES // 2
PERIODS_PER_BATCH = TILES_PER_BATCH // 2
UNITS = 2 * TILES
UNITS_PER_PERIOD = 4
UNITS_PER_BATCH = 2 * TILES_PER_BATCH

PRODUCT_LAG = 2
TILES_STORED_BY_HALVES = 2
LAST_ON_VECTOR = 4
TRANSPOSES_AHEAD = 2
VECTOR_COLUMNS = 336
LAST_TRANSPOSE_STEP = UNITS_PER_PERIOD * (PERIODS - 1 - TRANSPOSES_AHEAD)


def unit_order():
    first_batch = [(i, h) for h in range(2) for i in range(TILES_PER_BATCH)]
    return first_batch + [(i, h) for i in range(TILES_PER_BATCH, TILES) for h in range(2)]


def product_on_gpsimd(n):
    if n < TILES_PER_BATCH:
        return n in (0, 2, 4)
    if n < LAST_TRANSPOSE_STEP:
        return n % 8 in (1, 4, 7)
    return n % 2 == 0 and n < UNITS - LAST_ON_VECTOR


def tile_splatinformationflow_pb_kernel(
    tc, token_embeddings, splat_influences, decoded, gate_W, gate_b, out
):
    nc = tc.nc
    with ExitStack() as ctx:
        const = ctx.enter_context(tc.tile_pool(name="const", bufs=1))
        tokens_in = ctx.enter_context(tc.tile_pool(name="tokens_in", bufs=PERIODS))
        per_batch = ctx.enter_context(tc.tile_pool(name="per_batch", bufs=BATCHES))
        weights_in = ctx.enter_context(tc.tile_pool(name="weights_in", bufs=2 * PASSES))
        codes = ctx.enter_context(tc.tile_pool(name="codes", bufs=6))
        epilogue = ctx.enter_context(tc.tile_pool(name="epilogue", bufs=8))
        psum = ctx.enter_context(tc.psum_pool(name="psum", bufs=3))
        ctx.enter_context(tc.manual_schedule())

        tokens_view = [token_embeddings[b].rearrange("(p c) k -> p c k", c=TILES_PER_BATCH) for b in range(BATCHES)]
        influences_view = [splat_influences[b].rearrange("(p c) s -> p c s", c=TILES_PER_BATCH) for b in range(BATCHES)]
        out_view = [out[b].rearrange("(p c) n -> p c n", c=TILES_PER_BATCH) for b in range(BATCHES)]

        tokens, influences, influences_t, states = {}, {}, {}, {}
        weights_raw, weights_grouped = {}, {}
        words_t, tokens_grouped, token_codes, token_scales = {}, {}, {}, {}
        z_banks, flow_banks, gates, results = {}, {}, {}, {}
        held_products = []
        halves_done = {}

        warm = const.tile([P, 1], F32, name="warm")
        nc.vector.memset(warm[:], 0.0)
        nc.scalar.activation(out=warm[:], in_=warm[:], func=SIGMOID)
        identity_f32 = const.tile([P, P], F32, name="identity_f32")
        masks.make_identity(nc, identity_f32[:])
        identity_bf16 = const.tile([P, P], BF16, name="identity_bf16")
        masks.make_identity(nc, identity_bf16[:])
        ones = const.tile([P, P], BF16, name="ones")
        nc.vector.memset(ones[:], 1.0)
        bias_row = const.tile([P, FEATURES], BF16, name="bias_row")
        nc.vector.memset(bias_row[:], 0.0)
        bias = const.tile([P, FEATURES], F32, name="bias")
        weight_codes = const.tile([P, PASSES, FEATURES], U32, name="weight_codes", align_bytes=64)
        weight_scales = const.tile([P, PASSES, FEATURES], U8, name="weight_scales", align_bytes=64)
        turnstile = const.tile([P, 1], U32, name="turnstile")

        def gpsimd_waits_for(code_words):
            nc.gpsimd.tensor_copy(out=turnstile[:], in_=code_words)

        def half_columns(h):
            return slice(HALF * h, HALF * (h + 1))

        def load_tokens(j):
            b, c = (2 * j) // TILES_PER_BATCH, (2 * j) % TILES_PER_BATCH
            raw = tokens_in.tile([P, 2, FEATURES], BF16, name="tokens", tag="tokens")
            nc.sync.dma_start(out=raw[:], in_=tokens_view[b][:, c : c + 2, :])
            tokens[j] = raw

        def load_weights(g, h):
            raw = weights_in.tile([P, PACK, HALF], BF16, name="weights_raw", tag="weights_raw")
            rows = gate_W[K_PASS * g : K_PASS * (g + 1), half_columns(h)]
            nc.sync.dma_start(out=raw[:], in_=rows.rearrange("(p j) n -> p j n", j=PACK))
            weights_raw[(g, h)] = raw

        def load_batch(b):
            raw = per_batch.tile([P, TILES_PER_BATCH, SPLATS], BF16, name="influences", tag="influences")
            nc.sync.dma_start(out=raw[:], in_=influences_view[b])
            influences[b] = raw
            state = per_batch.tile([P, FEATURES], BF16, name="states", tag="states")
            nc.sync.dma_start(out=state[:], in_=decoded[b])
            states[b] = state

        def interleave_weights(g, h):
            raw = weights_raw[(g, h)]
            grouped = weights_in.tile([P, HALF, PACK], BF16, name="weights_grouped", tag="weights_grouped", bufs=2, align_bytes=64)
            v = VECTOR_COLUMNS
            nc.vector.tensor_copy(
                out=grouped[:, :v, :].rearrange("p (c i) j -> p c j i", i=4), in_=raw[:, :, :v].rearrange("p j (c i) -> p c j i", i=4)
            )
            nc.scalar.copy(
                out=grouped[:, v:, :].rearrange("p (c i) j -> p c j i", i=4), in_=raw[:, :, v:].rearrange("p j (c i) -> p c j i", i=4)
            )
            gpsimd_waits_for(grouped[:, 0, 0:2].bitcast(U32))
            weights_grouped[(g, h)] = grouped

        def quantize_weights(g, h):
            nc.vector.quantize_mx(
                out=weight_codes[:, g, half_columns(h)].bitcast(E5M2_X4),
                scales=weight_scales[:, g, half_columns(h)],
                in_=weights_grouped[(g, h)][:].rearrange("p n j -> p (n j)"),
            )
            gpsimd_waits_for(weight_codes[:, g, HALF * h : HALF * h + 1])

        def transpose_tokens(j):
            for t in range(2):
                bank = psum.tile([P, PASSES, 2, P], F32, name="words_t", tag="words_t", bufs=2)
                words = tokens[j][:, t, :].bitcast(F32)
                for g in range(PASSES):
                    for u in range(2):
                        nc.tensor.transpose(bank[:, g, u, :], words[:, WORDS_PER_PASS * g + u : WORDS_PER_PASS * (g + 1) : 2], identity_f32[:])
                words_t[(j, t)] = bank

        def regroup_tokens(j, t, copy):
            if t == 0:
                fresh = codes.tile([P, 2, FEATURES], BF16, name="tokens_grouped", tag="tokens_grouped", bufs=3, align_bytes=64)
                tokens_grouped[j] = fresh
            copy(
                out=tokens_grouped[j][:, t, :].bitcast(F32).rearrange("p (g r u) -> p g r u", g=PASSES, u=2),
                in_=words_t[(j, t)][:].rearrange("p g u r -> p g r u"),
            )

        def quantize_tokens(j):
            packed = codes.tile([P, 2 * PASSES * P], U32, name="token_codes", tag="token_codes", align_bytes=64)
            scale_bytes = codes.tile([P, 2 * PASSES * P], U8, name="token_scales", tag="token_scales", align_bytes=64)
            nc.vector.quantize_mx(
                out=packed[:].bitcast(E5M2_X4), scales=scale_bytes[:], in_=tokens_grouped[j][:].rearrange("p t c -> p (t c)")
            )
            gpsimd_waits_for(packed[:, 0:1])
            token_codes[j] = packed
            token_scales[j] = scale_bytes

        def transpose_influences(b):
            bank = psum.tile([P, TILES_PER_BATCH, P], BF16, name="influences_bank", tag="flow")
            for c in range(TILES_PER_BATCH):
                nc.tensor.transpose(bank[:, c, :], influences[b][:, c, :], identity_bf16[:])
            turned = per_batch.tile([P, TILES_PER_BATCH, P], BF16, name="influences_t", tag="influences_t")
            nc.scalar.copy(out=turned[:], in_=bank[:])
            influences_t[b] = turned

        def spread_bias():
            for h in range(2):
                bank = psum.tile([P, HALF], F32, name="bias_bank", tag="z")
                nc.tensor.matmul(out=bank[:], lhsT=ones[:], rhs=bias_row[:, half_columns(h)], start=True, stop=True)
                nc.scalar.copy(out=bias[:, half_columns(h)], in_=bank[:])

        def gate_matmul(unit):
            i, h = unit
            j, t = i // 2, i % 2
            bank = psum.tile([P, HALF], F32, name="z", tag="z")
            for g in range(PASSES):
                token_columns = slice((PASSES * t + g) * P, (PASSES * t + g + 1) * P)
                nc.tensor.matmul_mx(
                    out=bank[:],
                    lhsT=token_codes[j][:, token_columns].bitcast(E5M2_X4),
                    lhsT_scale=token_scales[j][:, token_columns],
                    rhs=weight_codes[:, g, half_columns(h)].bitcast(E5M2_X4),
                    rhs_scale=weight_scales[:, g, half_columns(h)],
                    start=(g == 0),
                    stop=(g == PASSES - 1),
                )
            z_banks[unit] = bank

        def flow_matmul(unit):
            i, h = unit
            b, c = i // TILES_PER_BATCH, i % TILES_PER_BATCH
            bank = psum.tile([P, HALF], F32, name="flow", tag="flow")
            nc.tensor.matmul(out=bank[:], lhsT=influences_t[b][:, c, :], rhs=states[b][:, half_columns(h)], start=True, stop=True)
            flow_banks[unit] = bank

        def add_bias(unit):
            gate = epilogue.tile([P, HALF], F32, name="gate", tag="gate")
            nc.vector.tensor_tensor(out=gate[:], in0=z_banks[unit][:], in1=bias[:, half_columns(unit[1])], op=ADD)
            gates[unit] = gate

        def sigmoid(unit):
            nc.scalar.activation(out=gates[unit][:], in_=gates[unit][:], func=SIGMOID)

        def product(unit, on_gpsimd):
            i, h = unit
            if i not in results:
                fresh = epilogue.tile([P, FEATURES], F32, name="result", tag="result", bufs=10)
                results[i] = fresh
            target = results[i][:, half_columns(h)]
            if on_gpsimd:
                flow = epilogue.tile([P, HALF], F32, name="flow_copy", tag="flow_copy", bufs=3)
                nc.scalar.copy(out=flow[:], in_=flow_banks[unit][:])
                held_products.append((unit, target, gates[unit], flow))
            else:
                nc.vector.tensor_tensor(out=target, in0=flow_banks[unit][:], in1=gates[unit][:], op=MULT)
                store_what_is_whole(unit)

        def release_products():
            for unit, target, gate, flow in held_products:
                nc.gpsimd.tensor_tensor(out=target, in0=gate[:], in1=flow[:], op=MULT)
                store_what_is_whole(unit)
            held_products.clear()

        def store(i, columns):
            b, c = i // TILES_PER_BATCH, i % TILES_PER_BATCH
            nc.sync.dma_start(out=out_view[b][:, c, columns], in_=results[i][:, columns])

        def store_what_is_whole(unit):
            i, h = unit
            halves_done[i] = halves_done.get(i, 0) + 1
            if i >= TILES - TILES_STORED_BY_HALVES:
                store(i, half_columns(h))
            elif halves_done[i] == 2:
                store(i, slice(0, FEATURES))

        load_tokens(0)
        load_weights(0, 0)
        load_weights(1, 0)
        load_tokens(1)
        nc.sync.dma_start(out=bias_row[0:1, :], in_=gate_b.rearrange("(o n) -> o n", o=1))
        load_batch(0)
        load_tokens(2)
        load_tokens(3)
        load_weights(0, 1)
        load_weights(1, 1)
        load_tokens(4)
        load_tokens(5)
        load_batch(1)
        for j in range(6, PERIODS):
            if j % PERIODS_PER_BATCH == 0:
                load_batch(j // PERIODS_PER_BATCH)
            load_tokens(j)

        transpose_tokens(0)
        regroup_tokens(0, 0, nc.vector.tensor_copy)
        regroup_tokens(0, 1, nc.scalar.copy)
        interleave_weights(0, 0)
        interleave_weights(1, 0)
        quantize_weights(0, 0)
        quantize_tokens(0)
        quantize_weights(1, 0)
        transpose_tokens(1)
        regroup_tokens(1, 0, nc.scalar.copy)
        regroup_tokens(1, 1, nc.scalar.copy)
        spread_bias()
        quantize_tokens(1)

        units = unit_order()
        transposed_at = {}
        for j in range(2, PERIODS):
            transposed_at[2 * j - 3 if j < PERIODS_PER_BATCH else UNITS_PER_PERIOD * (j - TRANSPOSES_AHEAD)] = j
        right_half_at = {1: 0, 4: 1}
        last_weight_step = max(right_half_at) + 1

        for n in range(UNITS + PRODUCT_LAG):
            unit = units[n] if n < UNITS else None
            behind = units[n - PRODUCT_LAG] if n >= PRODUCT_LAG else None

            passes_first = n < TILES_PER_BATCH
            if passes_first:
                gate_matmul(unit)
                if n == 0:
                    transpose_influences(0)
            if n in transposed_at:
                j = transposed_at[n]
                transpose_tokens(j)
                if j % PERIODS_PER_BATCH == 0:
                    transpose_influences(j // PERIODS_PER_BATCH)
                regroup_tokens(j, 0, nc.scalar.copy)
                regroup_tokens(j, 1, nc.scalar.copy)

            if unit is not None and not passes_first:
                gate_matmul(unit)
            if behind is not None:
                flow_matmul(behind)
            if unit is not None:
                add_bias(unit)
            if transposed_at.get(n - 2, 0) >= PERIODS_PER_BATCH:
                quantize_tokens(transposed_at[n - 2])
            if behind is not None:
                product(behind, product_on_gpsimd(n - PRODUCT_LAG))
            if n > last_weight_step and transposed_at.get(n - 1, 0) < PERIODS_PER_BATCH:
                release_products()
            if unit is not None:
                sigmoid(unit)
            if 0 < transposed_at.get(n - 1, 0) < PERIODS_PER_BATCH:
                quantize_tokens(transposed_at[n - 1])
            if n in right_half_at:
                interleave_weights(right_half_at[n], 1)
            if n - 1 in right_half_at:
                quantize_weights(right_half_at[n - 1], 1)
            if n == last_weight_step:
                release_products()
